import numpy as np
import ml_dtypes


def mxq(x, axis, fmt="e4m3"):
    dtype, down = {"e4m3": (ml_dtypes.float8_e4m3fn, 7), "e5m2": (ml_dtypes.float8_e5m2, 14)}[fmt]
    v = np.moveaxis(np.asarray(x, np.float32).astype(ml_dtypes.bfloat16).astype(np.float64), axis, -1)
    blocks = v.reshape(v.shape[:-1] + (-1, 32))
    amax = np.abs(blocks).max(-1, keepdims=True)
    byte = np.maximum(np.where(amax > 0, np.frexp(amax)[1] - 1 + 127, 0) - down, 1)
    scale = np.exp2(byte - 127.0)
    codes = (blocks / scale).astype(np.float32).astype(dtype).astype(np.float64)
    return np.moveaxis((codes * scale).reshape(v.shape), -1, axis)


WIDE = False


def mx_kscale(k):
    if not WIDE:
        return np.ones(k)
    levels = np.array([18, -18])
    if k % 512:
        return np.exp2(np.random.permutation(np.resize(levels, k // 32))).repeat(32)
    a = np.empty((k // 512, 16))
    for p in range(k // 512):
        a[p, :8] = np.random.permutation(np.resize(levels, 8))
        for g in range(8):
            far = levels[np.abs(levels - a[p, g]) >= 10]
            a[p, g + 8] = far[np.random.randint(len(far))]
    return np.exp2(a.ravel()).repeat(32)


BF16 = ml_dtypes.bfloat16


def bf(x):
    return np.asarray(x, np.float32).astype(BF16)


def f64(x):
    return np.asarray(x).astype(np.float64)


B, S, D, C = 1024, 4, 512, 1024
MIN_SCALE = 1e-3
TEMPERATURE = 1.5


def sigmoid(v):
    return 1.0 / (1.0 + np.exp(-v))


def setup_inputs():
    u = mx_kscale(C)
    v = mx_kscale(D)
    s = mx_kscale(B)
    features0 = bf(np.random.standard_normal((B, D)) * 0.3)
    W_diag0 = bf(np.random.standard_normal((D, D)) * 2.0 / np.sqrt(D))
    b_diag = bf(-4.0 + 0.2 * np.random.standard_normal(D))
    W_cls0 = bf(np.random.standard_normal((C, D)) * 3.0 / np.sqrt(D))
    b_cls = bf(np.random.standard_normal(C) * 0.3)
    noise0 = bf(np.random.standard_normal((B, S, D)) * 10.0)
    lr_samples = bf(np.random.standard_normal((B, S, D)) * 0.3)
    g = bf(np.random.standard_normal((B, S, C)) * np.exp2(np.random.randint(-6, 1, (B, S, 1))) / s[:, None, None] * u)
    z = f64(features0) @ f64(W_diag0).T + f64(b_diag)
    return {
        "features": bf(f64(features0) * s[:, None]),
        "W_diag": bf(f64(W_diag0) / v[:, None]),
        "b_diag": b_diag,
        "W_cls": bf(f64(W_cls0) / u[:, None]),
        "b_cls": b_cls,
        "noise_diag": bf(f64(noise0) * v),
        "lr_samples": lr_samples,
        "z": np.asarray(z, np.float32),
        "grad_out": g,
    }


def reference(features, W_diag, b_diag, W_cls, b_cls, noise_diag, lr_samples, z, grad_out):
    dlogits = (f64(grad_out) / TEMPERATURE).reshape(-1, C)
    dpre = mxq(dlogits, 1, "e5m2") @ mxq(f64(W_cls), 0, "e4m3")
    dpre = dpre.reshape(-1, S, D)
    dstd = np.sum(dpre * f64(noise_diag), axis=1)
    dz = dstd * sigmoid(f64(z))
    direct = np.sum(dpre, axis=1)
    dfeatures = (mxq(dz, 1, "e5m2") @ mxq(f64(W_diag), 0, "e4m3")) + direct
    dW_diag = mxq(dz, 0, "e5m2").T @ mxq(f64(features), 0, "e4m3")
    return dfeatures, dW_diag

@@ -1,0 +1,397 @@
+from contextlib import ExitStack
+
+import concourse.mybir as mybir
+from concourse.masks import make_identity
+
+F32 = mybir.dt.float32
+BF16 = mybir.dt.bfloat16
+U32 = mybir.dt.uint32
+U8 = mybir.dt.uint8
+E4M3 = mybir.dt.float8_e4m3fn_x4
+E5M2 = mybir.dt.float8_e5m2_x4
+MULT = mybir.AluOpType.mult
+ADD = mybir.AluOpType.add
+
+P = 128
+B, S, D, C = 1024, 4, 512, 1024
+TEMPERATURE = 1.5
+TILES = B // P
+FLOPS = 2 * (B * S * C * D + B * D * D + D * D * B)
+BYTES = 2 * (B * S * C + B * S * D + B * D + D * D + C * D) + 4 * (B * D) + 4 * (B * D + D * D)
+
+
+def tile_hetxlhead_pa_v_kernel(
+    tc, features, w_diag, b_diag, w_cls, b_cls, noise_diag, lr_samples, z, grad_out, out_0, out_1
+):
+    nc = tc.nc
+    g_view = grad_out.rearrange("(g p j) s c -> g j p s c", p=P, j=4)
+    n_view = noise_diag.rearrange("(g p j) s d -> g j p s d", p=P, j=4)
+    z_view = z.rearrange("(g p j) d -> g j p d", p=P, j=4)
+    o_view = out_0.rearrange("(g p j) d -> g j p d", p=P, j=4)
+
+    with ExitStack() as ctx:
+        pool = ctx.enter_context(tc.tile_pool(name="sbuf", bufs=1))
+        psum = ctx.enter_context(tc.psum_pool(name="psum", bufs=1))
+
+        def sb(tag, shape, dtype, bufs):
+            return pool.tile(shape, dtype, name=tag, tag=tag, bufs=bufs, align_bytes=64)
+
+        def ps(tag, shape, bufs):
+            return psum.tile(shape, F32, name=tag, tag=tag, bufs=bufs)
+
+        ident = sb("ident", [P, P], F32, 1)
+        make_identity(nc, ident[:])
+
+        raw, noise, zt, gs, trb, grp, cod, dpb = {}, {}, {}, {}, {}, {}, {}, {}
+        prod, part, dstd, sig, dz, dzt_b, dzt, dzc, outb = {}, {}, {}, {}, {}, {}, {}, {}, {}
+
+        def quantised(tag, cols, bufs):
+            return sb(tag + "_c", [P, cols], U32, bufs), sb(tag + "_s", [P, cols], U8, bufs)
+
+        def load_g(J, hf, a=0, b=2):
+            if a == 0:
+                raw[J, hf] = sb("raw", [P, 2 * C], BF16, 12)
+            nc.sync.dma_start(
+                out=raw[J, hf][:, C * a : C * b].rearrange("p (s c) -> p s c", c=C),
+                in_=g_view[J // 4, J % 4][:, 2 * hf + a : 2 * hf + b, :],
+            )
+
+        def load_n(J):
+            noise[J] = sb("noise", [P, S, D], BF16, 5)
+            nc.sync.dma_start(out=noise[J][:], in_=n_view[J // 4, J % 4])
+
+        def load_z(J):
+            zt[J] = sb("z", [P, D], F32, 5)
+            nc.sync.dma_start(out=zt[J][:], in_=z_view[J // 4, J % 4])
+
+        def load_w(src):
+            t = sb("wraw", [P, 4, D], BF16, 3)
+            nc.sync.dma_start(out=t[:], in_=src.rearrange("(p j) w -> p j w", j=4))
+            return t
+
+        def prescale(J, hf, a=0, b=2):
+            if a == 0:
+                gs[J, hf] = sb("gs", [P, 2, 512, 2], BF16, 4)
+            nc.vector.tensor_scalar(
+                out=gs[J, hf][:, :, 256 * a : 256 * b, :],
+                in0=raw[J, hf][:, C * a : C * b].rearrange("p (q u e) -> p u q e", u=2, e=2),
+                scalar1=1.0 / TEMPERATURE,
+                scalar2=None,
+                op0=MULT,
+            )
+
+        def turn(J, s):
+            trb[J, s] = ps("tr", [P, 2, 2, P], 4)
+            words = gs[J, s // 2][:].rearrange("p u q e -> p (u q e)").bitcast(F32)
+            for h in range(2):
+                for u in range(2):
+                    a = u * 512 + (s % 2) * 256 + h * 128
+                    nc.tensor.transpose(trb[J, s][:, h, u, :], words[:, a : a + 128], ident[:])
+
+        def empty_turn(J, s):
+            hf = s // 2
+            if s % 2 == 0:
+                grp[J, hf] = sb("grp", [P, 2, 2, P, 2], F32, 3)
+            nc.scalar.copy(out=grp[J, hf][:, s % 2], in_=trb[J, s][:].rearrange("p h u r -> p h r u"))
+
+        def quant_g(J, hf, a=0, b=2):
+            if a == 0:
+                cod[J, hf] = quantised("g", 512, 8)
+            cols = slice(256 * a, 256 * b)
+            nc.vector.quantize_mx(
+                out=cod[J, hf][0][:, cols].bitcast(E5M2),
+                scales=cod[J, hf][1][:, cols],
+                in_=grp[J, hf][:, a:b].rearrange("p s h r u -> p (s h r u)").bitcast(BF16),
+            )
+
+        def g_pass(out, J, s, h, start, stop):
+            codes, scales = cod[J, s // 2]
+            cols = slice(((s % 2) * 2 + h) * P, ((s % 2) * 2 + h + 1) * P)
+            nc.tensor.matmul_mx(
+                out=out, lhsT=codes[:, cols].bitcast(E5M2), lhsT_scale=scales[:, cols],
+                rhs=wc[h][0][:].bitcast(E4M3), rhs_scale=wc[h][1][:], start=start, stop=stop,
+            )
+
+        def dpre(J, s):
+            dpb[J, s] = ps("dp", [P, D], 3)
+            for h in range(2):
+                g_pass(dpb[J, s][:], J, s, h, h == 0, h == 1)
+
+        def direct(J, s):
+            if s == 0:
+                outb[J] = ps("out", [P, D], 1) if J < TILES - 2 else ps("tr", [P, D], 4)
+            for h in range(2):
+                g_pass(outb[J][:], J, s, h, s == 0 and h == 0, False)
+
+        def times_noise(J, s):
+            hf = s // 2
+            if s % 2 == 0:
+                prod[J, hf] = sb("prod", [P, 2, D], F32, 4)
+            nc.vector.tensor_tensor(
+                out=prod[J, hf][:, s % 2, :], in0=dpb[J, s][:], in1=noise[J][:, s, :], op=MULT
+            )
+
+        def add_pair(J, hf):
+            part[J, hf] = sb("part", [P, D], F32, 3)
+            nc.vector.tensor_tensor(
+                out=part[J, hf][:], in0=prod[J, hf][:, 0, :], in1=prod[J, hf][:, 1, :], op=ADD
+            )
+
+        def add_all(J, eng):
+            dstd[J] = sb("dstd", [P, D], F32, 2)
+            eng.tensor_tensor(out=dstd[J][:], in0=part[J, 0][:], in1=part[J, 1][:], op=ADD)
+
+        def sigmoid(J):
+            sig[J] = sb("sig", [P, D], F32, 3)
+            nc.scalar.activation(sig[J][:], zt[J][:], mybir.ActivationFunctionType.Sigmoid)
+
+        def make_dz(J, cols, eng):
+            if J % 4 == 0 and cols.start == 0:
+                dz[J // 4] = sb("dz", [P, 4, D], BF16, 2)
+            eng.tensor_tensor(
+                out=dz[J // 4][:, J % 4, cols], in0=dstd[J][:, cols], in1=sig[J][:, cols], op=MULT
+            )
+
+        def turn_dz(J):
+            dzt_b[J] = ps("dp", [P, 2, P], 3)
+            words = dz[J // 4][:, J % 4, :].bitcast(F32)
+            for u in range(2):
+                nc.tensor.transpose(dzt_b[J][:, u, :], words[:, u : 256 : 2], ident[:])
+
+        def empty_dz(J):
+            dzt[J] = sb("dzt", [P, P, 2], F32, 2)
+            nc.scalar.copy(out=dzt[J][:], in_=dzt_b[J][:].rearrange("p u r -> p r u"))
+
+        def quant_dz(J):
+            dzc[J] = quantised("dzt", P, 2)
+            nc.vector.quantize_mx(
+                out=dzc[J][0][:].bitcast(E5M2), scales=dzc[J][1][:],
+                in_=dzt[J][:].rearrange("p r u -> p (r u)").bitcast(BF16),
+            )
+
+        def dz_pass(J):
+            nc.tensor.matmul_mx(
+                out=outb[J][:], lhsT=dzc[J][0][:].bitcast(E5M2), lhsT_scale=dzc[J][1][:],
+                rhs=wd[0][:].bitcast(E4M3), rhs_scale=wd[1][:], start=False, stop=True,
+            )
+
+        def store_out(J):
+            res = sb("res", [P, D], F32, 3)
+            nc.scalar.copy(out=res[:], in_=outb[J][:])
+            nc.sync.dma_start(out=o_view[J // 4, J % 4], in_=res[:])
+
+        def interleave(eng_copy, dst, src, cols):
+            eng_copy(out=dst[:, cols, :], in_=src[:, :, cols].rearrange("p j w -> p w j"))
+
+        def quant_w(pair, t, fmt, cols=slice(0, D)):
+            nc.vector.quantize_mx(
+                out=pair[0][:, cols].bitcast(fmt), scales=pair[1][:, cols],
+                in_=t[:, cols, :].rearrange("p w j -> p (w j)"),
+            )
+
+        def grouped_w():
+            return sb("wg", [P, D, 4], BF16, 2)
+
+        def weight_pass(m, g):
+            cols = slice(m * P, (m + 1) * P)
+            nc.tensor.matmul_mx(
+                out=acc[m][:], lhsT=dzq[g][0][:, cols].bitcast(E5M2), lhsT_scale=dzq[g][1][:, cols],
+                rhs=ft[g][0][:].bitcast(E4M3), rhs_scale=ft[g][1][:], start=g == 0, stop=g == 1,
+            )
+
+        full = slice(0, D)
+        left, right = slice(0, D // 2), slice(D // 2, D)
+        ctx.enter_context(tc.manual_schedule())
+
+        dummy = sb("dummy", [P, 1], F32, 1)
+        nc.vector.memset(dummy[:], 0.0)
+        nc.scalar.activation(dummy[:], dummy[:], mybir.ActivationFunctionType.Sigmoid)
+
+        load_g(0, 0, 0, 1)
+        wc_raw = [load_w(w_cls[0:512, :]), load_w(w_cls[512:1024, :])]
+        load_g(0, 0, 1, 2)
+        load_g(0, 1)
+        load_n(0)
+        for J in range(1, 5):
+            load_g(J, 0)
+            load_g(J, 1)
+            load_n(J)
+            if J == 1:
+                load_z(0)
+            load_z(J)
+            if J == 2:
+                wd_raw = load_w(w_diag)
+
+        wc = [quantised("wc0", D, 1), quantised("wc1", D, 1)]
+        wd = quantised("wd", D, 1)
+        ft = [quantised("ft0", D, 1), quantised("ft1", D, 1)]
+        dzq = [quantised("dz0", D, 1), quantised("dz1", D, 1)]
+
+        prescale(0, 0, 0, 1)
+        turn(0, 0)
+        empty_turn(0, 0)
+        wg = [grouped_w(), grouped_w()]
+        interleave(nc.vector.tensor_copy, wg[0], wc_raw[0], full)
+        interleave(nc.scalar.copy, wg[1], wc_raw[1], right)
+        quant_w(wc[0], wg[0], E4M3)
+        prescale(0, 0, 1, 2)
+        quant_g(0, 0, 0, 1)
+        turn(0, 1)
+        empty_turn(0, 1)
+        interleave(nc.vector.tensor_copy, wg[1], wc_raw[1], left)
+        prescale(0, 1)
+        turn(0, 2)
+        turn(0, 3)
+        empty_turn(0, 2)
+        empty_turn(0, 3)
+        quant_w(wc[1], wg[1], E4M3)
+        quant_g(0, 0, 1, 2)
+        dpre(0, 0)
+        dpre(0, 1)
+        prescale(1, 0)
+        times_noise(0, 0)
+        times_noise(0, 1)
+        turn(1, 0)
+        turn(1, 1)
+        quant_g(0, 1)
+        empty_turn(1, 0)
+        empty_turn(1, 1)
+        prescale(1, 1)
+        dpre(0, 2)
+        dpre(0, 3)
+        turn(1, 2)
+        turn(1, 3)
+        times_noise(0, 2)
+        times_noise(0, 3)
+        empty_turn(1, 2)
+        empty_turn(1, 3)
+        quant_g(1, 0)
+        prescale(2, 0)
+        turn(2, 0)
+        turn(2, 1)
+        quant_g(1, 1)
+        prescale(2, 1)
+        add_pair(0, 0)
+        sigmoid(0)
+        add_pair(0, 1)
+
+        ft_raw = [load_w(features[0:512, :]), load_w(features[512:1024, :])]
+        for J in range(5, TILES):
+            load_g(J, 0)
+            load_g(J, 1)
+            load_n(J)
+            load_z(J)
+
+        L = TILES - 1
+        acc = []
+        for J in range(1, TILES):
+            nxt = J + 1 < TILES
+            if nxt:
+                empty_turn(J + 1, 0)
+                empty_turn(J + 1, 1)
+            dpre(J, 0)
+            times_noise(J, 0)
+            if J < L:
+                add_all(J - 1, nc.gpsimd)
+            make_dz(J - 1, full, nc.gpsimd)
+            dpre(J, 1)
+            times_noise(J, 1)
+            if J >= 2:
+                dz_pass(J - 2)
+                store_out(J - 2)
+            if nxt and J > 1:
+                empty_turn(J + 1, 2)
+                empty_turn(J + 1, 3)
+            sigmoid(J)
+            if J == 1:
+                turn(2, 2)
+                turn(2, 3)
+            dpre(J, 2)
+            times_noise(J, 2)
+            if J == L:
+                direct(J - 1, 0)
+                direct(J - 1, 1)
+            dpre(J, 3)
+            if J == L:
+                add_pair(J, 0)
+            times_noise(J, 3)
+            if J == 1:
+                empty_turn(2, 2)
+                empty_turn(2, 3)
+            for s in range(2 if J == L else 0, S):
+                direct(J - 1, s)
+            if J + 2 < TILES:
+                prescale(J + 2, 0)
+                prescale(J + 2, 1)
+            if nxt:
+                quant_g(J + 1, 0)
+                add_pair(J, 0)
+                quant_g(J + 1, 1)
+            turn_dz(J - 1)
+            if J + 2 < TILES:
+                for s in range(S):
+                    turn(J + 2, s)
+            if J == L:
+                break
+            if J in (1, 2, 3, 5):
+                src = {1: wd_raw, 2: ft_raw[0], 3: ft_raw[1], 5: dz[0]}[J]
+                pair = {1: wd, 2: ft[0], 3: ft[1], 5: dzq[0]}[J]
+                t = grouped_w()
+                interleave(nc.scalar.copy, t, src, left)
+                empty_dz(J - 1)
+                interleave(nc.scalar.copy, t, src, right)
+                quant_dz(J - 1)
+                add_pair(J, 1)
+                quant_w(pair, t, E5M2 if J == 5 else E4M3)
+            else:
+                empty_dz(J - 1)
+                quant_dz(J - 1)
+                add_pair(J, 1)
+                if J == L - 1:
+                    add_all(J, nc.vector)
+                    acc = [ps("tr", [P, D], 4), ps("tr", [P, D], 4)]
+                    weight_pass(0, 0)
+                    weight_pass(1, 0)
+
+        part[L, 1] = sb("part", [P, D], F32, 3)
+        nc.vector.tensor_tensor(out=part[L, 1][:], in0=part[L, 0][:], in1=prod[L, 1][:, 0, :], op=ADD)
+        empty_dz(L - 1)
+        for s in range(S):
+            direct(L, s)
+        dstd[L] = sb("dstd", [P, D], F32, 2)
+        for cols in (left, right):
+            nc.vector.tensor_tensor(
+                out=dstd[L][:, cols], in0=part[L, 1][:, cols], in1=prod[L, 1][:, 1, cols], op=ADD
+            )
+        for cols in (left, right):
+            make_dz(L, cols, nc.vector)
+        acc += [ps("dp", [P, D], 3), ps("dp", [P, D], 3)]
+        turn_dz(L)
+        weight_pass(2, 0)
+        weight_pass(3, 0)
+        t = grouped_w()
+        quarter = [slice(m * P, (m + 1) * P) for m in range(4)]
+        interleave(nc.vector.tensor_copy, t, dz[1], quarter[0])
+        interleave(nc.scalar.copy, t, dz[1], quarter[1])
+        quant_dz(L - 1)
+        dz_pass(L - 1)
+        interleave(nc.vector.tensor_copy, t, dz[1], quarter[2])
+        quant_w(dzq[1], t, E5M2, quarter[0])
+        interleave(nc.vector.tensor_copy, t, dz[1], quarter[3])
+        quant_w(dzq[1], t, E5M2, quarter[1])
+        empty_dz(L)
+        quant_w(dzq[1], t, E5M2, quarter[2])
+        quant_w(dzq[1], t, E5M2, quarter[3])
+        quant_dz(L)
+        for m in range(4):
+            weight_pass(m, 1)
+        dz_pass(L)
+        store_out(L - 1)
+        for m in range(4):
+            r = sb("res1", [P, D], F32, 4)
+            if m % 2 == 0:
+                nc.vector.tensor_copy(out=r[:], in_=acc[m][:])
+            else:
+                nc.scalar.copy(out=r[:], in_=acc[m][:])
+            nc.sync.dma_start(out=out_1[m * P : (m + 1) * P, :], in_=r[:])
+        store_out(L)

@@ -42,6 +42,8 @@ def tile_hetxlhead_pa_v_kernel(
         ident = sb("ident", [P, P], F32, 1)
         make_identity(nc, ident[:])
 
+        SPLIT = (6, 7)
+        last = {}
         raw, noise, zt, gs, trb, grp, cod, dpb = {}, {}, {}, {}, {}, {}, {}, {}
         prod, part, dstd, sig, dz, dzt_b, dzt, dzc, outb = {}, {}, {}, {}, {}, {}, {}, {}, {}
 
@@ -78,6 +80,13 @@ def tile_hetxlhead_pa_v_kernel(
                 scalar1=1.0 / TEMPERATURE,
                 scalar2=None,
                 op0=MULT,
+            )
+
+        def scalar_prescale(J, hf):
+            gs[J, hf] = sb("gs", [P, 2, 512, 2], BF16, 4)
+            nc.scalar.activation(
+                gs[J, hf][:], raw[J, hf][:].rearrange("p (q u e) -> p u q e", u=2, e=2),
+                mybir.ActivationFunctionType.Copy, scale=1.0 / TEMPERATURE,
             )
 
         def turn(J, s):
@@ -118,6 +127,8 @@ def tile_hetxlhead_pa_v_kernel(
                 g_pass(dpb[J, s][:], J, s, h, h == 0, h == 1)
 
         def direct(J, s):
+            if s == 3 and J in SPLIT:
+                return
             if s == 0:
                 outb[J] = ps("out", [P, D], 1) if J < TILES - 2 else ps("tr", [P, D], 4)
             for h in range(2):
@@ -175,9 +186,17 @@ def tile_hetxlhead_pa_v_kernel(
                 rhs=wd[0][:].bitcast(E4M3), rhs_scale=wd[1][:], start=False, stop=True,
             )
 
+        def keep_last(J):
+            if J in SPLIT:
+                last[J] = sb("last", [P, D], F32, 2)
+                nc.scalar.copy(out=last[J][:], in_=dpb[J, 3][:])
+
         def store_out(J):
             res = sb("res", [P, D], F32, 3)
-            nc.scalar.copy(out=res[:], in_=outb[J][:])
+            if J in SPLIT:
+                nc.vector.tensor_tensor(out=res[:], in0=outb[J][:], in1=last[J][:], op=ADD)
+            else:
+                nc.scalar.copy(out=res[:], in_=outb[J][:])
             nc.sync.dma_start(out=o_view[J // 4, J % 4], in_=res[:])
 
         def interleave(eng_copy, dst, src, cols):
@@ -207,85 +226,130 @@ def tile_hetxlhead_pa_v_kernel(
         nc.vector.memset(dummy[:], 0.0)
         nc.scalar.activation(dummy[:], dummy[:], mybir.ActivationFunctionType.Sigmoid)
 
-        load_g(0, 0, 0, 1)
         wc_raw = [load_w(w_cls[0:512, :]), load_w(w_cls[512:1024, :])]
+        load_g(0, 0, 0, 1)
         load_g(0, 0, 1, 2)
         load_g(0, 1)
         load_n(0)
-        for J in range(1, 5):
+        load_g(1, 0)
+        load_g(1, 1)
+        load_z(0)
+        load_g(2, 0)
+        load_n(1)
+        load_g(2, 1)
+        load_z(1)
+        wd_raw = load_w(w_diag)
+        load_n(2)
+        for J in range(3, 5):
             load_g(J, 0)
             load_g(J, 1)
+            load_z(J - 1)
             load_n(J)
-            if J == 1:
-                load_z(0)
-            load_z(J)
-            if J == 2:
-                wd_raw = load_w(w_diag)
 
         wc = [quantised("wc0", D, 1), quantised("wc1", D, 1)]
         wd = quantised("wd", D, 1)
         ft = [quantised("ft0", D, 1), quantised("ft1", D, 1)]
         dzq = [quantised("dz0", D, 1), quantised("dz1", D, 1)]
 
+        wg = [grouped_w(), grouped_w()]
+        for h in range(2):
+            interleave(nc.vector.tensor_copy, wg[h], wc_raw[h], left)
+            interleave(nc.scalar.copy, wg[h], wc_raw[h], right)
         prescale(0, 0, 0, 1)
         turn(0, 0)
         empty_turn(0, 0)
-        wg = [grouped_w(), grouped_w()]
-        interleave(nc.vector.tensor_copy, wg[0], wc_raw[0], full)
-        interleave(nc.scalar.copy, wg[1], wc_raw[1], right)
         quant_w(wc[0], wg[0], E4M3)
         prescale(0, 0, 1, 2)
-        quant_g(0, 0, 0, 1)
         turn(0, 1)
+        quant_w(wc[1], wg[1], E4M3)
+        quant_g(0, 0, 0, 1)
         empty_turn(0, 1)
-        interleave(nc.vector.tensor_copy, wg[1], wc_raw[1], left)
         prescale(0, 1)
+        dpre(0, 0)
         turn(0, 2)
         turn(0, 3)
+        quant_g(0, 0, 1, 2)
         empty_turn(0, 2)
         empty_turn(0, 3)
-        quant_w(wc[1], wg[1], E4M3)
-        quant_g(0, 0, 1, 2)
-        dpre(0, 0)
         dpre(0, 1)
-        prescale(1, 0)
         times_noise(0, 0)
-        times_noise(0, 1)
+        prescale(1, 0)
         turn(1, 0)
         turn(1, 1)
+        times_noise(0, 1)
         quant_g(0, 1)
         empty_turn(1, 0)
         empty_turn(1, 1)
-        prescale(1, 1)
         dpre(0, 2)
         dpre(0, 3)
+        prescale(1, 1)
+        add_pair(0, 0)
         turn(1, 2)
         turn(1, 3)
         times_noise(0, 2)
         times_noise(0, 3)
         empty_turn(1, 2)
         empty_turn(1, 3)
+        sigmoid(0)
         quant_g(1, 0)
+        direct(0, 0)
+        direct(0, 1)
         prescale(2, 0)
+        dpre(1, 0)
         turn(2, 0)
         turn(2, 1)
-        quant_g(1, 1)
         prescale(2, 1)
-        add_pair(0, 0)
-        sigmoid(0)
+        empty_turn(2, 0)
+        empty_turn(2, 1)
+        quant_g(1, 1)
         add_pair(0, 1)
 
         ft_raw = [load_w(features[0:512, :]), load_w(features[512:1024, :])]
         for J in range(5, TILES):
             load_g(J, 0)
             load_g(J, 1)
+            load_z(J - 1)
             load_n(J)
-            load_z(J)
+        load_z(TILES - 1)
 
         L = TILES - 1
         acc = []
-        for J in range(1, TILES):
-            nxt = J + 1 < TILES
+        EARLY = (4,)
+        SIDE = {2: "f0", 3: "f1", 5: "dz"}
+        add_all(0, nc.gpsimd)
+        make_dz(0, full, nc.gpsimd)
+        dpre(1, 1)
+        times_noise(1, 0)
+        times_noise(1, 1)
+        dpre(1, 2)
+        times_noise(1, 2)
+        dpre(1, 3)
+        times_noise(1, 3)
+        direct(0, 2)
+        direct(0, 3)
+        turn(2, 2)
+        turn(2, 3)
+        side = grouped_w()
+        interleave(nc.scalar.copy, side, wd_raw, left)
+        empty_turn(2, 2)
+        empty_turn(2, 3)
+        interleave(nc.scalar.copy, side, wd_raw, right)
+        turn_dz(0)
+        empty_dz(0)
+        prescale(3, 0)
+        quant_g(2, 0)
+        prescale(3, 1)
+        sigmoid(1)
+        add_pair(1, 0)
+        quant_dz(0)
+        quant_g(2, 1)
+        quant_w(wd, side, E4M3)
+        for s in range(S):
+            turn(3, s)
+        add_pair(1, 1)
+
+        for J in range(2, TILES):
+            nxt = J < L
             if nxt:
                 empty_turn(J + 1, 0)
                 empty_turn(J + 1, 1)
@@ -296,16 +360,15 @@ def tile_hetxlhead_pa_v_kernel(
             make_dz(J - 1, full, nc.gpsimd)
             dpre(J, 1)
             times_noise(J, 1)
-            if J >= 2:
+            if J < L:
                 dz_pass(J - 2)
                 store_out(J - 2)
-            if nxt and J > 1:
+            if nxt:
                 empty_turn(J + 1, 2)
                 empty_turn(J + 1, 3)
             sigmoid(J)
-            if J == 1:
-                turn(2, 2)
-                turn(2, 3)
+            if J in EARLY:
+                scalar_prescale(J + 3, 1)
             dpre(J, 2)
             times_noise(J, 2)
             if J == L:
@@ -313,16 +376,18 @@ def tile_hetxlhead_pa_v_kernel(
                 direct(J - 1, 1)
             dpre(J, 3)
             if J == L:
+                quant_dz(J - 2)
+                dz_pass(J - 2)
+                store_out(J - 2)
                 add_pair(J, 0)
             times_noise(J, 3)
-            if J == 1:
-                empty_turn(2, 2)
-                empty_turn(2, 3)
+            keep_last(J)
             for s in range(2 if J == L else 0, S):
                 direct(J - 1, s)
             if J + 2 < TILES:
                 prescale(J + 2, 0)
-                prescale(J + 2, 1)
+                if J - 1 not in EARLY:
+                    prescale(J + 2, 1)
             if nxt:
                 quant_g(J + 1, 0)
                 add_pair(J, 0)
@@ -333,25 +398,26 @@ def tile_hetxlhead_pa_v_kernel(
                     turn(J + 2, s)
             if J == L:
                 break
-            if J in (1, 2, 3, 5):
-                src = {1: wd_raw, 2: ft_raw[0], 3: ft_raw[1], 5: dz[0]}[J]
-                pair = {1: wd, 2: ft[0], 3: ft[1], 5: dzq[0]}[J]
-                t = grouped_w()
-                interleave(nc.scalar.copy, t, src, left)
+            if J in SIDE:
+                src = {"f0": ft_raw[0], "f1": ft_raw[1], "dz": dz[0]}[SIDE[J]]
+                pair = {"f0": ft[0], "f1": ft[1], "dz": dzq[0]}[SIDE[J]]
+                side = grouped_w()
+                interleave(nc.scalar.copy, side, src, left)
                 empty_dz(J - 1)
-                interleave(nc.scalar.copy, t, src, right)
+                interleave(nc.scalar.copy, side, src, right)
                 quant_dz(J - 1)
                 add_pair(J, 1)
-                quant_w(pair, t, E5M2 if J == 5 else E4M3)
+                quant_w(pair, side, E5M2 if SIDE[J] == "dz" else E4M3)
             else:
                 empty_dz(J - 1)
-                quant_dz(J - 1)
+                if J < L - 1:
+                    quant_dz(J - 1)
                 add_pair(J, 1)
-                if J == L - 1:
-                    add_all(J, nc.vector)
-                    acc = [ps("tr", [P, D], 4), ps("tr", [P, D], 4)]
-                    weight_pass(0, 0)
-                    weight_pass(1, 0)
+            if J == L - 1:
+                add_all(J, nc.vector)
+                acc = [ps("tr", [P, D], 4), ps("tr", [P, D], 4)]
+                weight_pass(0, 0)
+                weight_pass(1, 0)
 
         part[L, 1] = sb("part", [P, D], F32, 3)
         nc.vector.tensor_tensor(out=part[L, 1][:], in0=part[L, 0][:], in1=prod[L, 1][:, 0, :], op=ADD)
@@ -389,7 +455,7 @@ def tile_hetxlhead_pa_v_kernel(
         store_out(L - 1)
         for m in range(4):
             r = sb("res1", [P, D], F32, 4)
-            if m % 2 == 0:
+            if m == 0:
                 nc.vector.tensor_copy(out=r[:], in_=acc[m][:])
             else:
                 nc.scalar.copy(out=r[:], in_=acc[m][:])

@@ -25,8 +25,8 @@ def tile_hetxlhead_pa_v_kernel(
 ):
     nc = tc.nc
     g_view = grad_out.rearrange("(g p j) s c -> g j p s c", p=P, j=4)
-    n_view = noise_diag.rearrange("(g p j) s d -> g j p s d", p=P, j=4)
-    z_view = z.rearrange("(g p j) d -> g j p d", p=P, j=4)
+    n_view = noise_diag.rearrange("(g p j) s d -> g p j s d", p=P, j=4)
+    z_view = z.rearrange("(g p j) d -> g p j d", p=P, j=4)
     o_view = out_0.rearrange("(g p j) d -> g j p d", p=P, j=4)
 
     with ExitStack() as ctx:
@@ -50,33 +50,42 @@ def tile_hetxlhead_pa_v_kernel(
         def quantised(tag, cols, bufs):
             return sb(tag + "_c", [P, cols], U32, bufs), sb(tag + "_s", [P, cols], U8, bufs)
 
-        def load_g(J, hf, a=0, b=2):
-            if a == 0:
-                raw[J, hf] = sb("raw", [P, 2 * C], BF16, 12)
+        def load_g(J, a=0, b=S):
+            if J % 2 == 0 and a == 0:
+                raw[J // 2] = sb("raw", [P, 2 * S * C], BF16, 3)
+            at = S * C * (J % 2)
             nc.sync.dma_start(
-                out=raw[J, hf][:, C * a : C * b].rearrange("p (s c) -> p s c", c=C),
-                in_=g_view[J // 4, J % 4][:, 2 * hf + a : 2 * hf + b, :],
+                out=raw[J // 2][:, at + C * a : at + C * b].rearrange("p (s c) -> p s c", c=C),
+                in_=g_view[J // 4, J % 4][:, a:b, :],
             )
 
-        def load_n(J):
-            noise[J] = sb("noise", [P, S, D], BF16, 5)
-            nc.sync.dma_start(out=noise[J][:], in_=n_view[J // 4, J % 4])
+        def load_n(J, count):
+            if J % 2 == 0:
+                noise[J // 2] = sb("noise", [P, 2, S, D], BF16, 3)
+            at = J % 2
+            nc.sync.dma_start(
+                out=noise[J // 2][:, at : at + count], in_=n_view[J // 4][:, J % 4 : J % 4 + count]
+            )
 
         def load_z(J):
-            zt[J] = sb("z", [P, D], F32, 5)
-            nc.sync.dma_start(out=zt[J][:], in_=z_view[J // 4, J % 4])
+            zt[J // 2] = sb("z", [P, 2, D], F32, 3)
+            nc.sync.dma_start(out=zt[J // 2][:], in_=z_view[J // 4][:, J % 4 : J % 4 + 2])
 
         def load_w(src):
             t = sb("wraw", [P, 4, D], BF16, 3)
             nc.sync.dma_start(out=t[:], in_=src.rearrange("(p j) w -> p j w", j=4))
             return t
 
+        def rows(J, a, b):
+            at = S * C * (J % 2)
+            return raw[J // 2][:, at + C * a : at + C * b]
+
         def prescale(J, hf, a=0, b=2):
             if a == 0:
                 gs[J, hf] = sb("gs", [P, 2, 512, 2], BF16, 4)
             nc.vector.tensor_scalar(
                 out=gs[J, hf][:, :, 256 * a : 256 * b, :],
-                in0=raw[J, hf][:, C * a : C * b].rearrange("p (q u e) -> p u q e", u=2, e=2),
+                in0=rows(J, 2 * hf + a, 2 * hf + b).rearrange("p (q u e) -> p u q e", u=2, e=2),
                 scalar1=1.0 / TEMPERATURE,
                 scalar2=None,
                 op0=MULT,
@@ -85,7 +94,7 @@ def tile_hetxlhead_pa_v_kernel(
         def scalar_prescale(J, hf):
             gs[J, hf] = sb("gs", [P, 2, 512, 2], BF16, 4)
             nc.scalar.activation(
-                gs[J, hf][:], raw[J, hf][:].rearrange("p (q u e) -> p u q e", u=2, e=2),
+                gs[J, hf][:], rows(J, 2 * hf, 2 * hf + 2).rearrange("p (q u e) -> p u q e", u=2, e=2),
                 mybir.ActivationFunctionType.Copy, scale=1.0 / TEMPERATURE,
             )
 
@@ -139,7 +148,7 @@ def tile_hetxlhead_pa_v_kernel(
             if s % 2 == 0:
                 prod[J, hf] = sb("prod", [P, 2, D], F32, 4)
             nc.vector.tensor_tensor(
-                out=prod[J, hf][:, s % 2, :], in0=dpb[J, s][:], in1=noise[J][:, s, :], op=MULT
+                out=prod[J, hf][:, s % 2, :], in0=dpb[J, s][:], in1=noise[J // 2][:, J % 2, s, :], op=MULT
             )
 
         def add_pair(J, hf):
@@ -154,7 +163,7 @@ def tile_hetxlhead_pa_v_kernel(
 
         def sigmoid(J):
             sig[J] = sb("sig", [P, D], F32, 3)
-            nc.scalar.activation(sig[J][:], zt[J][:], mybir.ActivationFunctionType.Sigmoid)
+            nc.scalar.activation(sig[J][:], zt[J // 2][:, J % 2, :], mybir.ActivationFunctionType.Sigmoid)
 
         def make_dz(J, cols, eng):
             if J % 4 == 0 and cols.start == 0:
@@ -227,24 +236,21 @@ def tile_hetxlhead_pa_v_kernel(
         nc.scalar.activation(dummy[:], dummy[:], mybir.ActivationFunctionType.Sigmoid)
 
         wc_raw = [load_w(w_cls[0:512, :]), load_w(w_cls[512:1024, :])]
-        load_g(0, 0, 0, 1)
-        load_g(0, 0, 1, 2)
-        load_g(0, 1)
-        load_n(0)
-        load_g(1, 0)
-        load_g(1, 1)
+        load_g(0, 0, 1)
+        load_g(0, 1, 2)
+        load_g(0, 2, 4)
+        load_n(0, 1)
+        load_g(1, 0, 2)
+        load_g(1, 2, 4)
+        load_g(2)
+        load_n(1, 1)
         load_z(0)
-        load_g(2, 0)
-        load_n(1)
-        load_g(2, 1)
-        load_z(1)
+        load_g(3)
         wd_raw = load_w(w_diag)
-        load_n(2)
-        for J in range(3, 5):
-            load_g(J, 0)
-            load_g(J, 1)
-            load_z(J - 1)
-            load_n(J)
+        load_n(2, 2)
+        load_g(4)
+        load_z(2)
+        load_g(5)
 
         wc = [quantised("wc0", D, 1), quantised("wc1", D, 1)]
         wd = quantised("wd", D, 1)
@@ -303,20 +309,21 @@ def tile_hetxlhead_pa_v_kernel(
         empty_turn(2, 1)
         quant_g(1, 1)
         add_pair(0, 1)
+        add_all(0, nc.vector)
 
-        ft_raw = [load_w(features[0:512, :]), load_w(features[512:1024, :])]
-        for J in range(5, TILES):
-            load_g(J, 0)
-            load_g(J, 1)
-            load_z(J - 1)
-            load_n(J)
-        load_z(TILES - 1)
+        ft_raw = [load_w(features[0:512, :])]
+        load_n(4, 2)
+        load_g(6)
+        load_z(4)
+        ft_raw.append(load_w(features[512:1024, :]))
+        load_g(7)
+        load_n(6, 2)
+        load_z(6)
 
         L = TILES - 1
         acc = []
-        EARLY = (4,)
-        SIDE = {2: "f0", 3: "f1", 5: "dz"}
-        add_all(0, nc.gpsimd)
+        EARLY = ()
+        SIDE = {3: "f0", 4: "f1", 5: "dz"}
         make_dz(0, full, nc.gpsimd)
         dpre(1, 1)
         times_noise(1, 0)
@@ -329,24 +336,25 @@ def tile_hetxlhead_pa_v_kernel(
         direct(0, 3)
         turn(2, 2)
         turn(2, 3)
-        side = grouped_w()
-        interleave(nc.scalar.copy, side, wd_raw, left)
+        turn_dz(0)
         empty_turn(2, 2)
         empty_turn(2, 3)
+        side = grouped_w()
         interleave(nc.scalar.copy, side, wd_raw, right)
-        turn_dz(0)
         empty_dz(0)
         prescale(3, 0)
         quant_g(2, 0)
         prescale(3, 1)
         sigmoid(1)
         add_pair(1, 0)
-        quant_dz(0)
         quant_g(2, 1)
-        quant_w(wd, side, E4M3)
         for s in range(S):
             turn(3, s)
         add_pair(1, 1)
+        interleave(nc.vector.tensor_copy, side, wd_raw, left)
+        quant_dz(0)
+        quant_w(wd, side, E4M3)
+        add_all(1, nc.vector)
 
         for J in range(2, TILES):
             nxt = J < L
@@ -355,8 +363,6 @@ def tile_hetxlhead_pa_v_kernel(
                 empty_turn(J + 1, 1)
             dpre(J, 0)
             times_noise(J, 0)
-            if J < L:
-                add_all(J - 1, nc.gpsimd)
             make_dz(J - 1, full, nc.gpsimd)
             dpre(J, 1)
             times_noise(J, 1)
@@ -388,6 +394,8 @@ def tile_hetxlhead_pa_v_kernel(
                 prescale(J + 2, 0)
                 if J - 1 not in EARLY:
                     prescale(J + 2, 1)
+            if J - 1 in SIDE:
+                quant_w(pair, side, E5M2 if SIDE[J - 1] == "dz" else E4M3)
             if nxt:
                 quant_g(J + 1, 0)
                 add_pair(J, 0)
@@ -405,16 +413,15 @@ def tile_hetxlhead_pa_v_kernel(
                 interleave(nc.scalar.copy, side, src, left)
                 empty_dz(J - 1)
                 interleave(nc.scalar.copy, side, src, right)
-                quant_dz(J - 1)
                 add_pair(J, 1)
-                quant_w(pair, side, E5M2 if SIDE[J] == "dz" else E4M3)
+                quant_dz(J - 1)
             else:
                 empty_dz(J - 1)
+                add_pair(J, 1)
                 if J < L - 1:
                     quant_dz(J - 1)
-                add_pair(J, 1)
+            add_all(J, nc.vector)
             if J == L - 1:
-                add_all(J, nc.vector)
                 acc = [ps("tr", [P, D], 4), ps("tr", [P, D], 4)]
                 weight_pass(0, 0)
                 weight_pass(1, 0)

from contextlib import ExitStack

import concourse.mybir as mybir
from concourse.masks import make_identity

F32 = mybir.dt.float32
BF16 = mybir.dt.bfloat16
U32 = mybir.dt.uint32
U8 = mybir.dt.uint8
E4M3 = mybir.dt.float8_e4m3fn_x4
E5M2 = mybir.dt.float8_e5m2_x4
MULT = mybir.AluOpType.mult
ADD = mybir.AluOpType.add

P = 128
B, S, D, C = 1024, 4, 512, 1024
TEMPERATURE = 1.5
TILES = B // P
FLOPS = 2 * (B * S * C * D + B * D * D + D * D * B)
BYTES = 2 * (B * S * C + B * S * D + B * D + D * D + C * D) + 4 * (B * D) + 4 * (B * D + D * D)


def tile_hetxlhead_pa_v_kernel(
    tc, features, w_diag, b_diag, w_cls, b_cls, noise_diag, lr_samples, z, grad_out, out_0, out_1
):
    nc = tc.nc
    g_view = grad_out.rearrange("(g p j) s c -> g j p s c", p=P, j=4)
    n_view = noise_diag.rearrange("(g p j) s d -> g p j s d", p=P, j=4)
    z_view = z.rearrange("(g p j) d -> g p j d", p=P, j=4)
    o_view = out_0.rearrange("(g p j) d -> g j p d", p=P, j=4)

    with ExitStack() as ctx:
        pool = ctx.enter_context(tc.tile_pool(name="sbuf", bufs=1))
        psum = ctx.enter_context(tc.psum_pool(name="psum", bufs=1))

        def sb(tag, shape, dtype, bufs):
            return pool.tile(shape, dtype, name=tag, tag=tag, bufs=bufs, align_bytes=64)

        def ps(tag, shape, bufs):
            return psum.tile(shape, F32, name=tag, tag=tag, bufs=bufs)

        ident = sb("ident", [P, P], F32, 1)
        make_identity(nc, ident[:])

        SPLIT = (6, 7)
        last = {}
        raw, noise, zt, gs, trb, grp, cod, dpb = {}, {}, {}, {}, {}, {}, {}, {}
        prod, part, dstd, sig, dz, dzt_b, dzt, dzc, outb = {}, {}, {}, {}, {}, {}, {}, {}, {}

        def quantised(tag, cols, bufs):
            return sb(tag + "_c", [P, cols], U32, bufs), sb(tag + "_s", [P, cols], U8, bufs)

        def load_g(J, a=0, b=S):
            if J % 2 == 0 and a == 0:
                raw[J // 2] = sb("raw", [P, 2 * S * C], BF16, 3)
            at = S * C * (J % 2)
            nc.sync.dma_start(
                out=raw[J // 2][:, at + C * a : at + C * b].rearrange("p (s c) -> p s c", c=C),
                in_=g_view[J // 4, J % 4][:, a:b, :],
            )

        def load_n(J, count):
            if J % 2 == 0:
                noise[J // 2] = sb("noise", [P, 2, S, D], BF16, 3)
            at = J % 2
            nc.sync.dma_start(
                out=noise[J // 2][:, at : at + count], in_=n_view[J // 4][:, J % 4 : J % 4 + count]
            )

        def load_z(J):
            zt[J // 2] = sb("z", [P, 2, D], F32, 3)
            nc.sync.dma_start(out=zt[J // 2][:], in_=z_view[J // 4][:, J % 4 : J % 4 + 2])

        def load_w(src):
            t = sb("wraw", [P, 4, D], BF16, 3)
            nc.sync.dma_start(out=t[:], in_=src.rearrange("(p j) w -> p j w", j=4))
            return t

        def rows(J, a, b):
            at = S * C * (J % 2)
            return raw[J // 2][:, at + C * a : at + C * b]

        def prescale(J, hf, a=0, b=2):
            if a == 0:
                gs[J, hf] = sb("gs", [P, 2, 512, 2], BF16, 4)
            nc.vector.tensor_scalar(
                out=gs[J, hf][:, :, 256 * a : 256 * b, :],
                in0=rows(J, 2 * hf + a, 2 * hf + b).rearrange("p (q u e) -> p u q e", u=2, e=2),
                scalar1=1.0 / TEMPERATURE,
                scalar2=None,
                op0=MULT,
            )

        def scalar_prescale(J, hf):
            gs[J, hf] = sb("gs", [P, 2, 512, 2], BF16, 4)
            nc.scalar.activation(
                gs[J, hf][:], rows(J, 2 * hf, 2 * hf + 2).rearrange("p (q u e) -> p u q e", u=2, e=2),
                mybir.ActivationFunctionType.Copy, scale=1.0 / TEMPERATURE,
            )

        def turn(J, s):
            trb[J, s] = ps("tr", [P, 2, 2, P], 4)
            words = gs[J, s // 2][:].rearrange("p u q e -> p (u q e)").bitcast(F32)
            for h in range(2):
                for u in range(2):
                    a = u * 512 + (s % 2) * 256 + h * 128
                    nc.tensor.transpose(trb[J, s][:, h, u, :], words[:, a : a + 128], ident[:])

        def empty_turn(J, s):
            hf = s // 2
            if s % 2 == 0:
                grp[J, hf] = sb("grp", [P, 2, 2, P, 2], F32, 3)
            nc.scalar.copy(out=grp[J, hf][:, s % 2], in_=trb[J, s][:].rearrange("p h u r -> p h r u"))

        def quant_g(J, hf, a=0, b=2):
            if a == 0:
                cod[J, hf] = quantised("g", 512, 8)
            cols = slice(256 * a, 256 * b)
            nc.vector.quantize_mx(
                out=cod[J, hf][0][:, cols].bitcast(E5M2),
                scales=cod[J, hf][1][:, cols],
                in_=grp[J, hf][:, a:b].rearrange("p s h r u -> p (s h r u)").bitcast(BF16),
            )

        def g_pass(out, J, s, h, start, stop):
            codes, scales = cod[J, s // 2]
            cols = slice(((s % 2) * 2 + h) * P, ((s % 2) * 2 + h + 1) * P)
            nc.tensor.matmul_mx(
                out=out, lhsT=codes[:, cols].bitcast(E5M2), lhsT_scale=scales[:, cols],
                rhs=wc[h][0][:].bitcast(E4M3), rhs_scale=wc[h][1][:], start=start, stop=stop,
            )

        def dpre(J, s):
            dpb[J, s] = ps("dp", [P, D], 3)
            for h in range(2):
                g_pass(dpb[J, s][:], J, s, h, h == 0, h == 1)

        def direct(J, s):
            if s == 3 and J in SPLIT:
                return
            if s == 0:
                outb[J] = ps("out", [P, D], 1) if J < TILES - 2 else ps("tr", [P, D], 4)
            for h in range(2):
                g_pass(outb[J][:], J, s, h, s == 0 and h == 0, False)

        def times_noise(J, s):
            hf = s // 2
            if s % 2 == 0:
                prod[J, hf] = sb("prod", [P, 2, D], F32, 4)
            nc.vector.tensor_tensor(
                out=prod[J, hf][:, s % 2, :], in0=dpb[J, s][:], in1=noise[J // 2][:, J % 2, s, :], op=MULT
            )

        def add_pair(J, hf):
            part[J, hf] = sb("part", [P, D], F32, 3)
            nc.vector.tensor_tensor(
                out=part[J, hf][:], in0=prod[J, hf][:, 0, :], in1=prod[J, hf][:, 1, :], op=ADD
            )

        def add_all(J, eng):
            dstd[J] = sb("dstd", [P, D], F32, 2)
            eng.tensor_tensor(out=dstd[J][:], in0=part[J, 0][:], in1=part[J, 1][:], op=ADD)

        def sigmoid(J):
            sig[J] = sb("sig", [P, D], F32, 3)
            nc.scalar.activation(sig[J][:], zt[J // 2][:, J % 2, :], mybir.ActivationFunctionType.Sigmoid)

        def make_dz(J, cols, eng):
            if J % 4 == 0 and cols.start == 0:
                dz[J // 4] = sb("dz", [P, 4, D], BF16, 2)
            eng.tensor_tensor(
                out=dz[J // 4][:, J % 4, cols], in0=dstd[J][:, cols], in1=sig[J][:, cols], op=MULT
            )

        def turn_dz(J):
            dzt_b[J] = ps("dp", [P, 2, P], 3)
            words = dz[J // 4][:, J % 4, :].bitcast(F32)
            for u in range(2):
                nc.tensor.transpose(dzt_b[J][:, u, :], words[:, u : 256 : 2], ident[:])

        def empty_dz(J):
            dzt[J] = sb("dzt", [P, P, 2], F32, 2)
            nc.scalar.copy(out=dzt[J][:], in_=dzt_b[J][:].rearrange("p u r -> p r u"))

        def quant_dz(J):
            dzc[J] = quantised("dzt", P, 2)
            nc.vector.quantize_mx(
                out=dzc[J][0][:].bitcast(E5M2), scales=dzc[J][1][:],
                in_=dzt[J][:].rearrange("p r u -> p (r u)").bitcast(BF16),
            )

        def dz_pass(J):
            nc.tensor.matmul_mx(
                out=outb[J][:], lhsT=dzc[J][0][:].bitcast(E5M2), lhsT_scale=dzc[J][1][:],
                rhs=wd[0][:].bitcast(E4M3), rhs_scale=wd[1][:], start=False, stop=True,
            )

        def keep_last(J):
            if J in SPLIT:
                last[J] = sb("last", [P, D], F32, 2)
                nc.scalar.copy(out=last[J][:], in_=dpb[J, 3][:])

        def store_out(J):
            res = sb("res", [P, D], F32, 3)
            if J in SPLIT:
                nc.vector.tensor_tensor(out=res[:], in0=outb[J][:], in1=last[J][:], op=ADD)
            else:
                nc.scalar.copy(out=res[:], in_=outb[J][:])
            nc.sync.dma_start(out=o_view[J // 4, J % 4], in_=res[:])

        def interleave(eng_copy, dst, src, cols):
            eng_copy(out=dst[:, cols, :], in_=src[:, :, cols].rearrange("p j w -> p w j"))

        def quant_w(pair, t, fmt, cols=slice(0, D)):
            nc.vector.quantize_mx(
                out=pair[0][:, cols].bitcast(fmt), scales=pair[1][:, cols],
                in_=t[:, cols, :].rearrange("p w j -> p (w j)"),
            )

        def grouped_w():
            return sb("wg", [P, D, 4], BF16, 2)

        def weight_pass(m, g):
            cols = slice(m * P, (m + 1) * P)
            nc.tensor.matmul_mx(
                out=acc[m][:], lhsT=dzq[g][0][:, cols].bitcast(E5M2), lhsT_scale=dzq[g][1][:, cols],
                rhs=ft[g][0][:].bitcast(E4M3), rhs_scale=ft[g][1][:], start=g == 0, stop=g == 1,
            )

        full = slice(0, D)
        left, right = slice(0, D // 2), slice(D // 2, D)
        ctx.enter_context(tc.manual_schedule())

        dummy = sb("dummy", [P, 1], F32, 1)
        nc.vector.memset(dummy[:], 0.0)
        nc.scalar.activation(dummy[:], dummy[:], mybir.ActivationFunctionType.Sigmoid)

        wc_raw = [load_w(w_cls[0:512, :]), load_w(w_cls[512:1024, :])]
        load_g(0, 0, 1)
        load_g(0, 1, 2)
        load_g(0, 2, 4)
        load_n(0, 1)
        load_g(1, 0, 2)
        load_g(1, 2, 4)
        load_g(2)
        load_n(1, 1)
        load_z(0)
        load_g(3)
        wd_raw = load_w(w_diag)
        load_n(2, 2)
        load_g(4)
        load_z(2)
        load_g(5)

        wc = [quantised("wc0", D, 1), quantised("wc1", D, 1)]
        wd = quantised("wd", D, 1)
        ft = [quantised("ft0", D, 1), quantised("ft1", D, 1)]
        dzq = [quantised("dz0", D, 1), quantised("dz1", D, 1)]

        wg = [grouped_w(), grouped_w()]
        for h in range(2):
            interleave(nc.vector.tensor_copy, wg[h], wc_raw[h], left)
            interleave(nc.scalar.copy, wg[h], wc_raw[h], right)
        prescale(0, 0, 0, 1)
        turn(0, 0)
        empty_turn(0, 0)
        quant_w(wc[0], wg[0], E4M3)
        prescale(0, 0, 1, 2)
        turn(0, 1)
        quant_w(wc[1], wg[1], E4M3)
        quant_g(0, 0, 0, 1)
        empty_turn(0, 1)
        prescale(0, 1)
        dpre(0, 0)
        turn(0, 2)
        turn(0, 3)
        quant_g(0, 0, 1, 2)
        empty_turn(0, 2)
        empty_turn(0, 3)
        dpre(0, 1)
        times_noise(0, 0)
        prescale(1, 0)
        turn(1, 0)
        turn(1, 1)
        times_noise(0, 1)
        quant_g(0, 1)
        empty_turn(1, 0)
        empty_turn(1, 1)
        dpre(0, 2)
        dpre(0, 3)
        prescale(1, 1)
        add_pair(0, 0)
        turn(1, 2)
        turn(1, 3)
        times_noise(0, 2)
        times_noise(0, 3)
        empty_turn(1, 2)
        empty_turn(1, 3)
        sigmoid(0)
        quant_g(1, 0)
        direct(0, 0)
        direct(0, 1)
        prescale(2, 0)
        dpre(1, 0)
        turn(2, 0)
        turn(2, 1)
        prescale(2, 1)
        empty_turn(2, 0)
        empty_turn(2, 1)
        quant_g(1, 1)
        add_pair(0, 1)
        add_all(0, nc.vector)

        ft_raw = [load_w(features[0:512, :])]
        load_n(4, 2)
        load_g(6)
        load_z(4)
        ft_raw.append(load_w(features[512:1024, :]))
        load_g(7)
        load_n(6, 2)
        load_z(6)

        L = TILES - 1
        acc = []
        EARLY = ()
        SIDE = {3: "f0", 4: "f1", 5: "dz"}
        make_dz(0, full, nc.gpsimd)
        dpre(1, 1)
        times_noise(1, 0)
        times_noise(1, 1)
        dpre(1, 2)
        times_noise(1, 2)
        dpre(1, 3)
        times_noise(1, 3)
        direct(0, 2)
        direct(0, 3)
        turn(2, 2)
        turn(2, 3)
        turn_dz(0)
        empty_turn(2, 2)
        empty_turn(2, 3)
        side = grouped_w()
        interleave(nc.scalar.copy, side, wd_raw, right)
        empty_dz(0)
        prescale(3, 0)
        quant_g(2, 0)
        prescale(3, 1)
        sigmoid(1)
        add_pair(1, 0)
        quant_g(2, 1)
        for s in range(S):
            turn(3, s)
        add_pair(1, 1)
        interleave(nc.vector.tensor_copy, side, wd_raw, left)
        quant_dz(0)
        quant_w(wd, side, E4M3)
        add_all(1, nc.vector)

        for J in range(2, TILES):
            nxt = J < L
            if nxt:
                empty_turn(J + 1, 0)
                empty_turn(J + 1, 1)
            dpre(J, 0)
            times_noise(J, 0)
            make_dz(J - 1, full, nc.gpsimd)
            dpre(J, 1)
            times_noise(J, 1)
            if J < L:
                dz_pass(J - 2)
                store_out(J - 2)
            if nxt:
                empty_turn(J + 1, 2)
                empty_turn(J + 1, 3)
            sigmoid(J)
            if J in EARLY:
                scalar_prescale(J + 3, 1)
            dpre(J, 2)
            times_noise(J, 2)
            if J == L:
                direct(J - 1, 0)
                direct(J - 1, 1)
            dpre(J, 3)
            if J == L:
                quant_dz(J - 2)
                dz_pass(J - 2)
                store_out(J - 2)
                add_pair(J, 0)
            times_noise(J, 3)
            keep_last(J)
            for s in range(2 if J == L else 0, S):
                direct(J - 1, s)
            if J + 2 < TILES:
                prescale(J + 2, 0)
                if J - 1 not in EARLY:
                    prescale(J + 2, 1)
            if J - 1 in SIDE:
                quant_w(pair, side, E5M2 if SIDE[J - 1] == "dz" else E4M3)
            if nxt:
                quant_g(J + 1, 0)
                add_pair(J, 0)
                quant_g(J + 1, 1)
            turn_dz(J - 1)
            if J + 2 < TILES:
                for s in range(S):
                    turn(J + 2, s)
            if J == L:
                break
            if J in SIDE:
                src = {"f0": ft_raw[0], "f1": ft_raw[1], "dz": dz[0]}[SIDE[J]]
                pair = {"f0": ft[0], "f1": ft[1], "dz": dzq[0]}[SIDE[J]]
                side = grouped_w()
                interleave(nc.scalar.copy, side, src, left)
                empty_dz(J - 1)
                interleave(nc.scalar.copy, side, src, right)
                add_pair(J, 1)
                quant_dz(J - 1)
            else:
                empty_dz(J - 1)
                add_pair(J, 1)
                if J < L - 1:
                    quant_dz(J - 1)
            add_all(J, nc.vector)
            if J == L - 1:
                acc = [ps("tr", [P, D], 4), ps("tr", [P, D], 4)]
                weight_pass(0, 0)
                weight_pass(1, 0)

        part[L, 1] = sb("part", [P, D], F32, 3)
        nc.vector.tensor_tensor(out=part[L, 1][:], in0=part[L, 0][:], in1=prod[L, 1][:, 0, :], op=ADD)
        empty_dz(L - 1)
        for s in range(S):
            direct(L, s)
        dstd[L] = sb("dstd", [P, D], F32, 2)
        for cols in (left, right):
            nc.vector.tensor_tensor(
                out=dstd[L][:, cols], in0=part[L, 1][:, cols], in1=prod[L, 1][:, 1, cols], op=ADD
            )
        for cols in (left, right):
            make_dz(L, cols, nc.vector)
        acc += [ps("dp", [P, D], 3), ps("dp", [P, D], 3)]
        turn_dz(L)
        weight_pass(2, 0)
        weight_pass(3, 0)
        t = grouped_w()
        quarter = [slice(m * P, (m + 1) * P) for m in range(4)]
        interleave(nc.vector.tensor_copy, t, dz[1], quarter[0])
        interleave(nc.scalar.copy, t, dz[1], quarter[1])
        quant_dz(L - 1)
        dz_pass(L - 1)
        interleave(nc.vector.tensor_copy, t, dz[1], quarter[2])
        quant_w(dzq[1], t, E5M2, quarter[0])
        interleave(nc.vector.tensor_copy, t, dz[1], quarter[3])
        quant_w(dzq[1], t, E5M2, quarter[1])
        empty_dz(L)
        quant_w(dzq[1], t, E5M2, quarter[2])
        quant_w(dzq[1], t, E5M2, quarter[3])
        quant_dz(L)
        for m in range(4):
            weight_pass(m, 1)
        dz_pass(L)
        store_out(L - 1)
        for m in range(4):
            r = sb("res1", [P, D], F32, 4)
            if m == 0:
                nc.vector.tensor_copy(out=r[:], in_=acc[m][:])
            else:
                nc.scalar.copy(out=r[:], in_=acc[m][:])
            nc.sync.dma_start(out=out_1[m * P : (m + 1) * P, :], in_=r[:])
        store_out(L)
